import numpy as np
import ml_dtypes


def mxq(x, axis, fmt="e4m3"):
    dtype, down = {"e4m3": (ml_dtypes.float8_e4m3fn, 7), "e5m2": (ml_dtypes.float8_e5m2, 14)}[fmt]
    v = np.moveaxis(np.asarray(x, np.float32).astype(ml_dtypes.bfloat16).astype(np.float64), axis, -1)
    blocks = v.reshape(v.shape[:-1] + (-1, 32))
    amax = np.abs(blocks).max(-1, keepdims=True)
    byte = np.maximum(np.where(amax > 0, np.frexp(amax)[1] - 1 + 127, 0) - down, 1)
    scale = np.exp2(byte - 127.0)
    codes = (blocks / scale).astype(np.float32).astype(dtype).astype(np.float64)
    return np.moveaxis((codes * scale).reshape(v.shape), -1, axis)


WIDE = False


def mx_kscale(k):
    if not WIDE:
        return np.ones(k)
    levels = np.array([10, -10, 5, -5, 0])
    a = np.random.permutation(np.resize(levels, k // 512 * 4)).reshape(k // 512, 4)
    idx = np.arange(k)
    return np.exp2(a[idx // 512, idx % 128 // 32])


BF16 = ml_dtypes.bfloat16


def bf(x):
    return np.asarray(x, np.float32).astype(BF16)


def f64(x):
    return np.asarray(x).astype(np.float64)


NK, F, B = 3072, 512, 128
D = 2 * F
EPS = 1e-8


def rotate_half(x):
    d = x.shape[-1] // 2
    return np.concatenate([-x[..., d:], x[..., :d]], axis=-1)


def setup_inputs():
    sf = mx_kscale(F)
    s = np.concatenate([sf, sf])
    c = np.exp2(np.round(0.5 * np.log2(np.mean(1.0 / s**2))))
    return {"K": bf(np.random.standard_normal((NK, D)) * s * c),
            "reference_angles": bf(np.random.random(F) * 2.0 * np.pi),
            "probes": bf(np.random.standard_normal((B, D)) / s),
            "u_weights": bf(np.random.standard_normal((B, F)) * 0.5 / np.sqrt(F) / (sf * c)),
            "k_bias": bf(np.random.standard_normal(B) * 0.5)}


def reference(K, reference_angles, probes, u_weights, k_bias):
    K = f64(K)
    probes = f64(probes)
    pnorm = np.sqrt(np.sum(probes**2, axis=-1, keepdims=True))
    p = probes / (pnorm + EPS)
    theta_full = np.concatenate([f64(reference_angles), f64(reference_angles)], axis=-1)
    rotated = p * np.cos(theta_full) + rotate_half(p) * np.sin(theta_full)
    dot_term = mxq(K, 1, "e4m3") @ mxq(rotated, 1, "e4m3").T
    K_mag = np.sqrt(K[..., :F] ** 2 + K[..., F:] ** 2 + EPS)
    logits = dot_term + (mxq(K_mag, 1, "e4m3") @ mxq(f64(u_weights), 1, "e4m3").T) + f64(k_bias)
    return logits

@@ -1,0 +1,255 @@
+import math
+from contextlib import ExitStack
+
+import concourse.mybir as mybir
+from concourse.masks import make_identity
+
+F32 = mybir.dt.float32
+BF16 = mybir.dt.bfloat16
+U32 = mybir.dt.uint32
+U8 = mybir.dt.uint8
+FP8X4 = mybir.dt.float8_e4m3fn_x4
+ACT = mybir.ActivationFunctionType
+ALU = mybir.AluOpType
+
+P = 128
+PACK = 4
+ROWS = 3072
+FREQS = 512
+FEATURES = 2 * FREQS
+ROW_TILES = ROWS // P
+PAIR = 2
+PAIRS = ROW_TILES // PAIR
+EPS = 1e-8
+
+FLOPS = 2 * ROWS * P * (FEATURES + FREQS)
+
+TWO_PI = 2.0 * math.pi
+TWO_PI_HIGH = 6.28125
+TWO_PI_LOW = TWO_PI - TWO_PI_HIGH
+ROUND_MAGIC = 1.5 * 2.0**23
+
+
+def quantise(nc, values, codes, scales):
+    nc.vector.quantize_mx(out=codes.bitcast(FP8X4), scales=scales, in_=values)
+
+
+def tile_module2network_kernel(tc, K, reference_angles, probes, u_weights, k_bias, out):
+    nc = tc.nc
+    with ExitStack() as ctx:
+        const = ctx.enter_context(tc.tile_pool(name="const", bufs=1))
+        k_pool = ctx.enter_context(tc.tile_pool(name="k_in", bufs=PAIRS))
+        mx_pool = ctx.enter_context(tc.tile_pool(name="mx", bufs=PAIRS))
+        work = ctx.enter_context(tc.tile_pool(name="work", bufs=3))
+        turned_pool = ctx.enter_context(tc.psum_pool(name="turned", bufs=6))
+        acc_pool = ctx.enter_context(tc.psum_pool(name="acc", bufs=2))
+
+        theta = const.tile([P, PACK], BF16)
+        nc.sync.dma_start(
+            out=theta[:].rearrange("p (u e) -> p u e", u=2),
+            in_=reference_angles.rearrange("(u p e) -> p u e", u=2, e=2),
+        )
+        probes_sb = const.tile([P, FEATURES], BF16)
+        nc.sync.dma_start(out=probes_sb[:], in_=probes)
+        u_sb = const.tile([P, FREQS], BF16)
+        nc.sync.dma_start(out=u_sb[:], in_=u_weights)
+        bias_rows = const.tile([P, P], BF16)
+        nc.sync.dma_start(out=bias_rows[:], in_=k_bias.partition_broadcast(P))
+        k_rows = K.rearrange("(p j) k -> p j k", j=ROW_TILES)
+        k_in = []
+        for i in range(PAIRS):
+            k_pair = k_pool.tile([P, PAIR, FEATURES], BF16, name="k_pair")
+            nc.sync.dma_start(out=k_pair[:], in_=k_rows[:, PAIR * i : PAIR * (i + 1), :])
+            k_in.append(k_pair)
+
+        zero_col = const.tile([P, 1], F32)
+        nc.gpsimd.memset(zero_col[:], 0.0)
+        warm_col = const.tile([P, 1], F32)
+        nc.scalar.activation(out=warm_col[:], in_=zero_col[:], func=ACT.Sin)
+        ident = const.tile([P, P], F32)
+        make_identity(nc, ident[:])
+        eps_col = const.tile([P, 1], F32)
+        nc.gpsimd.memset(eps_col[:], EPS)
+
+        angle = const.tile([P, 2 * PACK], F32)
+        nc.vector.tensor_scalar(
+            out=angle[:, 0:PACK], in0=theta[:], scalar1=1.0, scalar2=0.0, op0=ALU.mult, op1=ALU.add
+        )
+        nc.vector.tensor_scalar(
+            out=angle[:, PACK : 2 * PACK],
+            in0=theta[:],
+            scalar1=1.0,
+            scalar2=0.5 * math.pi,
+            op0=ALU.mult,
+            op1=ALU.add,
+        )
+        turns = const.tile([P, 2 * PACK], F32)
+        nc.vector.tensor_scalar(
+            out=turns[:],
+            in0=angle[:],
+            scalar1=1.0 / TWO_PI,
+            scalar2=ROUND_MAGIC,
+            op0=ALU.mult,
+            op1=ALU.add,
+        )
+        off_high = const.tile([P, 2 * PACK], F32)
+        nc.vector.tensor_scalar(
+            out=off_high[:],
+            in0=turns[:],
+            scalar1=-ROUND_MAGIC,
+            scalar2=-TWO_PI_HIGH,
+            op0=ALU.add,
+            op1=ALU.mult,
+        )
+        off_low = const.tile([P, 2 * PACK], F32)
+        nc.vector.tensor_scalar(
+            out=off_low[:],
+            in0=turns[:],
+            scalar1=-ROUND_MAGIC,
+            scalar2=-TWO_PI_LOW,
+            op0=ALU.add,
+            op1=ALU.mult,
+        )
+        reduced_high = const.tile([P, 2 * PACK], F32)
+        nc.vector.tensor_tensor(out=reduced_high[:], in0=angle[:], in1=off_high[:], op=ALU.add)
+        reduced = const.tile([P, 2 * PACK], F32)
+        nc.vector.tensor_tensor(out=reduced[:], in0=reduced_high[:], in1=off_low[:], op=ALU.add)
+        sin_cos = const.tile([P, 2 * PACK], F32)
+        nc.scalar.activation(out=sin_cos[:], in_=reduced[:], func=ACT.Sin)
+        sin_b = sin_cos[:, 0:PACK].unsqueeze(2).to_broadcast([P, PACK, P])
+        cos_b = sin_cos[:, PACK : 2 * PACK].unsqueeze(2).to_broadcast([P, PACK, P])
+
+        squares = const.tile([P, FEATURES], BF16)
+        sum_squares = const.tile([P, 1], F32)
+        nc.scalar.activation(
+            out=squares[:], in_=probes_sb[:], func=ACT.Square, accum_out=sum_squares[:]
+        )
+        norm = const.tile([P, 1], F32)
+        nc.scalar.activation(out=norm[:], in_=sum_squares[:], func=ACT.Sqrt)
+        norm_eps = const.tile([P, 1], F32)
+        nc.vector.tensor_scalar_add(out=norm_eps[:], in0=norm[:], scalar1=EPS)
+        inv_norm = const.tile([P, 1], F32)
+        nc.vector.reciprocal(out=inv_norm[:], in_=norm_eps[:])
+        p_unit = const.tile([P, FEATURES], F32)
+        nc.vector.tensor_scalar_mul(out=p_unit[:], in0=probes_sb[:], scalar1=inv_norm[:, 0:1])
+
+        p_cols = p_unit[:].rearrange("b (g u q e) -> b g u q e", g=2, u=2, e=2)
+        p_turned = []
+        for g in range(2):
+            p_bank = turned_pool.tile([P, PACK, P], F32, tag="turned", name="p_bank")
+            for u in range(2):
+                for e in range(2):
+                    nc.tensor.transpose(p_bank[:, 2 * u + e, :], p_cols[:, g, u, :, e], ident[:])
+            p_turned.append(p_bank)
+
+        re_cos = const.tile([P, PACK, P], F32)
+        nc.vector.tensor_tensor(out=re_cos[:], in0=p_turned[0][:], in1=cos_b, op=ALU.mult)
+        im_sin = const.tile([P, PACK, P], F32)
+        nc.vector.tensor_tensor(out=im_sin[:], in0=p_turned[1][:], in1=sin_b, op=ALU.mult)
+        im_cos = const.tile([P, PACK, P], F32)
+        nc.vector.tensor_tensor(out=im_cos[:], in0=p_turned[1][:], in1=cos_b, op=ALU.mult)
+        re_sin = const.tile([P, PACK, P], F32)
+        nc.vector.tensor_tensor(out=re_sin[:], in0=p_turned[0][:], in1=sin_b, op=ALU.mult)
+        rot_grouped = const.tile([P, 2, P, PACK], BF16, align_bytes=64)
+        nc.vector.tensor_tensor(
+            out=rot_grouped[:, 0],
+            in0=re_cos[:].rearrange("p t b -> p b t"),
+            in1=im_sin[:].rearrange("p t b -> p b t"),
+            op=ALU.subtract,
+        )
+        nc.vector.tensor_tensor(
+            out=rot_grouped[:, 1],
+            in0=im_cos[:].rearrange("p t b -> p b t"),
+            in1=re_sin[:].rearrange("p t b -> p b t"),
+            op=ALU.add,
+        )
+        rot_codes = const.tile([P, 2, P], U32, align_bytes=64)
+        rot_scales = const.tile([P, 2, P], U8, align_bytes=64)
+        quantise(
+            nc,
+            rot_grouped[:].rearrange("p g b t -> p (g b t)"),
+            rot_codes[:].rearrange("p g b -> p (g b)"),
+            rot_scales[:].rearrange("p g b -> p (g b)"),
+        )
+
+        u_words = u_sb[:].bitcast(F32)
+        u_bank = turned_pool.tile([P, PACK, P], F32, tag="turned", name="u_bank")
+        for u in range(2):
+            nc.tensor.transpose(u_bank[:, u, :], u_words[:, P * u : P * (u + 1)], ident[:])
+        u_grouped = const.tile([P, P, PACK], BF16, align_bytes=64)
+        nc.vector.tensor_copy(
+            out=u_grouped[:].bitcast(F32), in_=u_bank[:, 0:2, :].rearrange("p u b -> p b u")
+        )
+        u_codes = const.tile([P, P], U32, align_bytes=64)
+        u_scales = const.tile([P, P], U8, align_bytes=64)
+        quantise(nc, u_grouped[:].rearrange("p b t -> p (b t)"), u_codes[:], u_scales[:])
+
+        out_rows = out.rearrange("(p j) b -> p j b", j=ROW_TILES)
+        bias_b = bias_rows[:].unsqueeze(1).to_broadcast([P, PAIR, P])
+        for i in range(PAIRS):
+            k_words = k_in[i][:].bitcast(F32)
+            k_grouped = work.tile([P, PAIR, 2, P, PACK], BF16, align_bytes=64)
+            k_grouped_words = k_grouped[:].bitcast(F32)
+            for j in range(PAIR):
+                k_bank = turned_pool.tile([P, PACK, P], F32, tag="turned", name="k_bank")
+                for c in range(PACK):
+                    nc.tensor.transpose(k_bank[:, c, :], k_words[:, j, P * c : P * (c + 1)], ident[:])
+                nc.vector.tensor_copy(
+                    out=k_grouped_words[:, j], in_=k_bank[:].rearrange("p (g u) n -> p g n u", g=2)
+                )
+            k_codes = mx_pool.tile([P, PAIR, 2, P], U32, align_bytes=64)
+            k_scales = mx_pool.tile([P, PAIR, 2, P], U8, align_bytes=64)
+            quantise(
+                nc,
+                k_grouped[:].rearrange("p j g n t -> p (j g n t)"),
+                k_codes[:].rearrange("p j g n -> p (j g n)"),
+                k_scales[:].rearrange("p j g n -> p (j g n)"),
+            )
+
+            k_squared = work.tile([P, PAIR, 2, P * PACK], F32)
+            nc.scalar.activation(
+                out=k_squared[:].rearrange("p j g w -> p (j g w)"),
+                in_=k_grouped[:].rearrange("p j g n t -> p (j g n t)"),
+                func=ACT.Square,
+            )
+            mag_squared = work.tile([P, PAIR, P * PACK], F32)
+            nc.vector.tensor_tensor(
+                out=mag_squared[:], in0=k_squared[:, :, 0, :], in1=k_squared[:, :, 1, :], op=ALU.add
+            )
+            mag_grouped = work.tile([P, PAIR, P * PACK], BF16, align_bytes=64)
+            nc.scalar.activation(
+                out=mag_grouped[:], in_=mag_squared[:], func=ACT.Sqrt, bias=eps_col[:, 0:1]
+            )
+            mag_codes = mx_pool.tile([P, PAIR, P], U32, align_bytes=64)
+            mag_scales = mx_pool.tile([P, PAIR, P], U8, align_bytes=64)
+            quantise(
+                nc,
+                mag_grouped[:].rearrange("p j w -> p (j w)"),
+                mag_codes[:].rearrange("p j n -> p (j n)"),
+                mag_scales[:].rearrange("p j n -> p (j n)"),
+            )
+
+            acc = acc_pool.tile([P, PAIR, P], F32)
+            for j in range(PAIR):
+                for g in range(2):
+                    nc.tensor.matmul_mx(
+                        out=acc[:, j, :],
+                        lhsT=k_codes[:, j, g, :].bitcast(FP8X4),
+                        lhsT_scale=k_scales[:, j, g, :],
+                        rhs=rot_codes[:, g, :].bitcast(FP8X4),
+                        rhs_scale=rot_scales[:, g, :],
+                        start=(g == 0),
+                        stop=False,
+                    )
+                nc.tensor.matmul_mx(
+                    out=acc[:, j, :],
+                    lhsT=mag_codes[:, j, :].bitcast(FP8X4),
+                    lhsT_scale=mag_scales[:, j, :],
+                    rhs=u_codes[:].bitcast(FP8X4),
+                    rhs_scale=u_scales[:],
+                    start=False,
+                    stop=True,
+                )
+            logits = work.tile([P, PAIR, P], F32)
+            nc.vector.tensor_tensor(out=logits[:], in0=acc[:], in1=bias_b, op=ALU.add)
+            nc.sync.dma_start(out=out_rows[:, PAIR * i : PAIR * (i + 1), :], in_=logits[:])

@@ -21,6 +21,8 @@ ROW_TILES = ROWS // P
 PAIR = 2
 PAIRS = ROW_TILES // PAIR
 EPS = 1e-8
+SCALAR_COLS = 640
+PRODUCT_LAG = 4
 
 FLOPS = 2 * ROWS * P * (FEATURES + FREQS)
 
@@ -41,8 +43,10 @@ def tile_module2network_kernel(tc, K, reference_angles, probes, u_weights, k_bia
         k_pool = ctx.enter_context(tc.tile_pool(name="k_in", bufs=PAIRS))
         mx_pool = ctx.enter_context(tc.tile_pool(name="mx", bufs=PAIRS))
         work = ctx.enter_context(tc.tile_pool(name="work", bufs=3))
-        turned_pool = ctx.enter_context(tc.psum_pool(name="turned", bufs=6))
+        k_bank_pool = ctx.enter_context(tc.psum_pool(name="k_bank", bufs=2))
+        mag_bank_pool = ctx.enter_context(tc.psum_pool(name="mag_bank", bufs=4))
         acc_pool = ctx.enter_context(tc.psum_pool(name="acc", bufs=2))
+        ctx.enter_context(tc.manual_schedule())
 
         theta = const.tile([P, PACK], BF16)
         nc.sync.dma_start(
@@ -51,16 +55,18 @@ def tile_module2network_kernel(tc, K, reference_angles, probes, u_weights, k_bia
         )
         probes_sb = const.tile([P, FEATURES], BF16)
         nc.sync.dma_start(out=probes_sb[:], in_=probes)
-        u_sb = const.tile([P, FREQS], BF16)
-        nc.sync.dma_start(out=u_sb[:], in_=u_weights)
-        bias_rows = const.tile([P, P], BF16)
-        nc.sync.dma_start(out=bias_rows[:], in_=k_bias.partition_broadcast(P))
         k_rows = K.rearrange("(p j) k -> p j k", j=ROW_TILES)
         k_in = []
         for i in range(PAIRS):
             k_pair = k_pool.tile([P, PAIR, FEATURES], BF16, name="k_pair")
-            nc.sync.dma_start(out=k_pair[:], in_=k_rows[:, PAIR * i : PAIR * (i + 1), :])
             k_in.append(k_pair)
+        nc.sync.dma_start(out=k_in[0][:], in_=k_rows[:, 0:PAIR, :])
+        u_sb = const.tile([P, FREQS], BF16)
+        nc.sync.dma_start(out=u_sb[:], in_=u_weights)
+        bias_rows = const.tile([P, P], BF16)
+        nc.sync.dma_start(out=bias_rows[:], in_=k_bias.partition_broadcast(P))
+        for i in range(1, PAIRS):
+            nc.sync.dma_start(out=k_in[i][:], in_=k_rows[:, PAIR * i : PAIR * (i + 1), :])
 
         zero_col = const.tile([P, 1], F32)
         nc.gpsimd.memset(zero_col[:], 0.0)
@@ -70,6 +76,157 @@ def tile_module2network_kernel(tc, K, reference_angles, probes, u_weights, k_bia
         make_identity(nc, ident[:])
         eps_col = const.tile([P, 1], F32)
         nc.gpsimd.memset(eps_col[:], EPS)
+
+        k_squared = {}
+        k_banks = {}
+        k_grouped = {}
+        k_codes = {}
+        k_scales = {}
+        mag_banks = {}
+        mag_grouped = {}
+        mag_codes = {}
+        mag_scales = {}
+        accs = {}
+        out_rows = out.rearrange("(p j) b -> p j b", j=ROW_TILES)
+        bias_b = bias_rows[:].unsqueeze(1).to_broadcast([P, PAIR, P])
+
+        def exists(i):
+            return 0 <= i < PAIRS
+
+        def squares(i):
+            if not exists(i):
+                return
+            k_squared[i] = work.tile([P, PAIR, FEATURES], F32, name="k_squared")
+            nc.scalar.activation(
+                out=k_squared[i][:, :, 0:SCALAR_COLS],
+                in_=k_in[i][:, :, 0:SCALAR_COLS],
+                func=ACT.Square,
+            )
+            nc.gpsimd.tensor_tensor(
+                out=k_squared[i][:, :, SCALAR_COLS:FEATURES],
+                in0=k_in[i][:, :, SCALAR_COLS:FEATURES],
+                in1=k_in[i][:, :, SCALAR_COLS:FEATURES],
+                op=ALU.mult,
+            )
+
+        def turn_k(i):
+            if not exists(i):
+                return
+            k_words = k_in[i][:].bitcast(F32)
+            k_banks[i] = []
+            for j in range(PAIR):
+                k_bank = k_bank_pool.tile([P, PACK, P], F32, name="k_bank")
+                for c in range(PACK):
+                    nc.tensor.transpose(k_bank[:, c, :], k_words[:, j, P * c : P * (c + 1)], ident[:])
+                k_banks[i].append(k_bank)
+
+        def copy_k(i):
+            if not exists(i):
+                return
+            k_grouped[i] = work.tile([P, PAIR, 2, P, PACK], BF16, align_bytes=64, name="k_grouped")
+            k_grouped_words = k_grouped[i][:].bitcast(F32)
+            for j in range(PAIR):
+                nc.vector.tensor_copy(
+                    out=k_grouped_words[:, j],
+                    in_=k_banks[i][j][:].rearrange("p (g u) n -> p g n u", g=2),
+                )
+
+        def quantise_k(i):
+            if not exists(i):
+                return
+            k_codes[i] = mx_pool.tile([P, PAIR, 2, P], U32, align_bytes=64, name="k_codes")
+            k_scales[i] = mx_pool.tile([P, PAIR, 2, P], U8, align_bytes=64, name="k_scales")
+            quantise(
+                nc,
+                k_grouped[i][:].rearrange("p j g n t -> p (j g n t)"),
+                k_codes[i][:].rearrange("p j g n -> p (j g n)"),
+                k_scales[i][:].rearrange("p j g n -> p (j g n)"),
+            )
+
+        def turn_squares(i):
+            if not exists(i):
+                return
+            mag_banks[i] = []
+            for j in range(PAIR):
+                mag_bank = mag_bank_pool.tile([P, PACK, P], F32, tag="mag_bank", name="mag_bank")
+                for t in range(PACK):
+                    for g in range(2):
+                        first = FREQS * g + P * t
+                        nc.tensor.matmul(
+                            out=mag_bank[:, t, :],
+                            lhsT=k_squared[i][:, j, first : first + P],
+                            rhs=ident[:],
+                            is_transpose=True,
+                            start=(g == 0),
+                            stop=(g == 1),
+                        )
+                mag_banks[i].append(mag_bank)
+
+        def roots(i):
+            if not exists(i):
+                return
+            mag_grouped[i] = work.tile([P, PAIR, P, PACK], BF16, align_bytes=64, name="mag_grouped")
+            for j in range(PAIR):
+                nc.scalar.activation(
+                    out=mag_grouped[i][:, j],
+                    in_=mag_banks[i][j][:].rearrange("p t n -> p n t"),
+                    func=ACT.Sqrt,
+                    bias=eps_col[:, 0:1],
+                )
+
+        def quantise_mag(i):
+            if not exists(i):
+                return
+            mag_codes[i] = mx_pool.tile([P, PAIR, P], U32, align_bytes=64, name="mag_codes")
+            mag_scales[i] = mx_pool.tile([P, PAIR, P], U8, align_bytes=64, name="mag_scales")
+            quantise(
+                nc,
+                mag_grouped[i][:].rearrange("p j n t -> p (j n t)"),
+                mag_codes[i][:].rearrange("p j n -> p (j n)"),
+                mag_scales[i][:].rearrange("p j n -> p (j n)"),
+            )
+
+        def products(i):
+            if not exists(i):
+                return
+            accs[i] = acc_pool.tile([P, PAIR, P], F32, tag="acc", name="acc")
+            for j in range(PAIR):
+                for g in range(2):
+                    nc.tensor.matmul_mx(
+                        out=accs[i][:, j, :],
+                        lhsT=k_codes[i][:, j, g, :].bitcast(FP8X4),
+                        lhsT_scale=k_scales[i][:, j, g, :],
+                        rhs=rot_codes[:, g, :].bitcast(FP8X4),
+                        rhs_scale=rot_scales[:, g, :],
+                        start=(g == 0),
+                        stop=False,
+                    )
+                nc.tensor.matmul_mx(
+                    out=accs[i][:, j, :],
+                    lhsT=mag_codes[i][:, j, :].bitcast(FP8X4),
+                    lhsT_scale=mag_scales[i][:, j, :],
+                    rhs=u_codes[:].bitcast(FP8X4),
+                    rhs_scale=u_scales[:],
+                    start=False,
+                    stop=True,
+                )
+
+        def finish(i):
+            if not exists(i):
+                return
+            logits = work.tile([P, PAIR, P], F32, name="logits")
+            nc.vector.tensor_tensor(out=logits[:], in0=accs[i][:], in1=bias_b, op=ALU.add)
+            nc.sync.dma_start(out=out_rows[:, PAIR * i : PAIR * (i + 1), :], in_=logits[:])
+
+        def step(s):
+            squares(s + 1)
+            turn_squares(s)
+            copy_k(s)
+            quantise_mag(s - 1)
+            turn_k(s + 1)
+            quantise_k(s)
+            roots(s)
+
 
         angle = const.tile([P, 2 * PACK], F32)
         nc.vector.tensor_scalar(
@@ -114,33 +271,53 @@ def tile_module2network_kernel(tc, K, reference_angles, probes, u_weights, k_bia
         nc.vector.tensor_tensor(out=reduced_high[:], in0=angle[:], in1=off_high[:], op=ALU.add)
         reduced = const.tile([P, 2 * PACK], F32)
         nc.vector.tensor_tensor(out=reduced[:], in0=reduced_high[:], in1=off_low[:], op=ALU.add)
+
+        probes_squared = const.tile([P, FEATURES], BF16)
+        sum_squares = const.tile([P, 1], F32)
+        nc.scalar.activation(
+            out=probes_squared[:], in_=probes_sb[:], func=ACT.Square, accum_out=sum_squares[:]
+        )
         sin_cos = const.tile([P, 2 * PACK], F32)
         nc.scalar.activation(out=sin_cos[:], in_=reduced[:], func=ACT.Sin)
         sin_b = sin_cos[:, 0:PACK].unsqueeze(2).to_broadcast([P, PACK, P])
         cos_b = sin_cos[:, PACK : 2 * PACK].unsqueeze(2).to_broadcast([P, PACK, P])
 
-        squares = const.tile([P, FEATURES], BF16)
-        sum_squares = const.tile([P, 1], F32)
-        nc.scalar.activation(
-            out=squares[:], in_=probes_sb[:], func=ACT.Square, accum_out=sum_squares[:]
-        )
+        step(-1)
+
         norm = const.tile([P, 1], F32)
         nc.scalar.activation(out=norm[:], in_=sum_squares[:], func=ACT.Sqrt)
+
+        step(0)
+
+        u_f32 = const.tile([P, FREQS], F32)
+        nc.gpsimd.tensor_scalar(
+            out=u_f32[:], in0=u_sb[:], scalar1=1.0, scalar2=0.0, op0=ALU.mult, op1=ALU.add
+        )
+        u_bank = mag_bank_pool.tile([P, PACK, P], F32, tag="mag_bank", name="u_bank")
+        for t in range(PACK):
+            nc.tensor.transpose(u_bank[:, t, :], u_f32[:, P * t : P * (t + 1)], ident[:])
+
         norm_eps = const.tile([P, 1], F32)
         nc.vector.tensor_scalar_add(out=norm_eps[:], in0=norm[:], scalar1=EPS)
         inv_norm = const.tile([P, 1], F32)
         nc.vector.reciprocal(out=inv_norm[:], in_=norm_eps[:])
         p_unit = const.tile([P, FEATURES], F32)
         nc.vector.tensor_scalar_mul(out=p_unit[:], in0=probes_sb[:], scalar1=inv_norm[:, 0:1])
-
         p_cols = p_unit[:].rearrange("b (g u q e) -> b g u q e", g=2, u=2, e=2)
         p_turned = []
         for g in range(2):
-            p_bank = turned_pool.tile([P, PACK, P], F32, tag="turned", name="p_bank")
+            p_bank = acc_pool.tile([P, PACK, P], F32, tag="acc", name="p_bank")
             for u in range(2):
                 for e in range(2):
                     nc.tensor.transpose(p_bank[:, 2 * u + e, :], p_cols[:, g, u, :, e], ident[:])
             p_turned.append(p_bank)
+        u_grouped = const.tile([P, P, PACK], BF16, align_bytes=64)
+        nc.vector.tensor_copy(out=u_grouped[:], in_=u_bank[:].rearrange("p t b -> p b t"))
+        u_codes = const.tile([P, P], U32, align_bytes=64)
+        u_scales = const.tile([P, P], U8, align_bytes=64)
+        quantise(nc, u_grouped[:].rearrange("p b t -> p (b t)"), u_codes[:], u_scales[:])
+
+        step(1)
 
         re_cos = const.tile([P, PACK, P], F32)
         nc.vector.tensor_tensor(out=re_cos[:], in0=p_turned[0][:], in1=cos_b, op=ALU.mult)
@@ -150,19 +327,25 @@ def tile_module2network_kernel(tc, K, reference_angles, probes, u_weights, k_bia
         nc.vector.tensor_tensor(out=im_cos[:], in0=p_turned[1][:], in1=cos_b, op=ALU.mult)
         re_sin = const.tile([P, PACK, P], F32)
         nc.vector.tensor_tensor(out=re_sin[:], in0=p_turned[0][:], in1=sin_b, op=ALU.mult)
+
+        step(2)
+
         rot_grouped = const.tile([P, 2, P, PACK], BF16, align_bytes=64)
-        nc.vector.tensor_tensor(
+        nc.gpsimd.tensor_tensor(
             out=rot_grouped[:, 0],
             in0=re_cos[:].rearrange("p t b -> p b t"),
             in1=im_sin[:].rearrange("p t b -> p b t"),
             op=ALU.subtract,
         )
-        nc.vector.tensor_tensor(
+        nc.gpsimd.tensor_tensor(
             out=rot_grouped[:, 1],
             in0=im_cos[:].rearrange("p t b -> p b t"),
             in1=re_sin[:].rearrange("p t b -> p b t"),
             op=ALU.add,
         )
+
+        step(3)
+
         rot_codes = const.tile([P, 2, P], U32, align_bytes=64)
         rot_scales = const.tile([P, 2, P], U8, align_bytes=64)
         quantise(
@@ -172,84 +355,7 @@ def tile_module2network_kernel(tc, K, reference_angles, probes, u_weights, k_bia
             rot_scales[:].rearrange("p g b -> p (g b)"),
         )
 
-        u_words = u_sb[:].bitcast(F32)
-        u_bank = turned_pool.tile([P, PACK, P], F32, tag="turned", name="u_bank")
-        for u in range(2):
-            nc.tensor.transpose(u_bank[:, u, :], u_words[:, P * u : P * (u + 1)], ident[:])
-        u_grouped = const.tile([P, P, PACK], BF16, align_bytes=64)
-        nc.vector.tensor_copy(
-            out=u_grouped[:].bitcast(F32), in_=u_bank[:, 0:2, :].rearrange("p u b -> p b u")
-        )
-        u_codes = const.tile([P, P], U32, align_bytes=64)
-        u_scales = const.tile([P, P], U8, align_bytes=64)
-        quantise(nc, u_grouped[:].rearrange("p b t -> p (b t)"), u_codes[:], u_scales[:])
-
-        out_rows = out.rearrange("(p j) b -> p j b", j=ROW_TILES)
-        bias_b = bias_rows[:].unsqueeze(1).to_broadcast([P, PAIR, P])
-        for i in range(PAIRS):
-            k_words = k_in[i][:].bitcast(F32)
-            k_grouped = work.tile([P, PAIR, 2, P, PACK], BF16, align_bytes=64)
-            k_grouped_words = k_grouped[:].bitcast(F32)
-            for j in range(PAIR):
-                k_bank = turned_pool.tile([P, PACK, P], F32, tag="turned", name="k_bank")
-                for c in range(PACK):
-                    nc.tensor.transpose(k_bank[:, c, :], k_words[:, j, P * c : P * (c + 1)], ident[:])
-                nc.vector.tensor_copy(
-                    out=k_grouped_words[:, j], in_=k_bank[:].rearrange("p (g u) n -> p g n u", g=2)
-                )
-            k_codes = mx_pool.tile([P, PAIR, 2, P], U32, align_bytes=64)
-            k_scales = mx_pool.tile([P, PAIR, 2, P], U8, align_bytes=64)
-            quantise(
-                nc,
-                k_grouped[:].rearrange("p j g n t -> p (j g n t)"),
-                k_codes[:].rearrange("p j g n -> p (j g n)"),
-                k_scales[:].rearrange("p j g n -> p (j g n)"),
-            )
-
-            k_squared = work.tile([P, PAIR, 2, P * PACK], F32)
-            nc.scalar.activation(
-                out=k_squared[:].rearrange("p j g w -> p (j g w)"),
-                in_=k_grouped[:].rearrange("p j g n t -> p (j g n t)"),
-                func=ACT.Square,
-            )
-            mag_squared = work.tile([P, PAIR, P * PACK], F32)
-            nc.vector.tensor_tensor(
-                out=mag_squared[:], in0=k_squared[:, :, 0, :], in1=k_squared[:, :, 1, :], op=ALU.add
-            )
-            mag_grouped = work.tile([P, PAIR, P * PACK], BF16, align_bytes=64)
-            nc.scalar.activation(
-                out=mag_grouped[:], in_=mag_squared[:], func=ACT.Sqrt, bias=eps_col[:, 0:1]
-            )
-            mag_codes = mx_pool.tile([P, PAIR, P], U32, align_bytes=64)
-            mag_scales = mx_pool.tile([P, PAIR, P], U8, align_bytes=64)
-            quantise(
-                nc,
-                mag_grouped[:].rearrange("p j w -> p (j w)"),
-                mag_codes[:].rearrange("p j n -> p (j n)"),
-                mag_scales[:].rearrange("p j n -> p (j n)"),
-            )
-
-            acc = acc_pool.tile([P, PAIR, P], F32)
-            for j in range(PAIR):
-                for g in range(2):
-                    nc.tensor.matmul_mx(
-                        out=acc[:, j, :],
-                        lhsT=k_codes[:, j, g, :].bitcast(FP8X4),
-                        lhsT_scale=k_scales[:, j, g, :],
-                        rhs=rot_codes[:, g, :].bitcast(FP8X4),
-                        rhs_scale=rot_scales[:, g, :],
-                        start=(g == 0),
-                        stop=False,
-                    )
-                nc.tensor.matmul_mx(
-                    out=acc[:, j, :],
-                    lhsT=mag_codes[:, j, :].bitcast(FP8X4),
-                    lhsT_scale=mag_scales[:, j, :],
-                    rhs=u_codes[:].bitcast(FP8X4),
-                    rhs_scale=u_scales[:],
-                    start=False,
-                    stop=True,
-                )
-            logits = work.tile([P, PAIR, P], F32)
-            nc.vector.tensor_tensor(out=logits[:], in0=acc[:], in1=bias_b, op=ALU.add)
-            nc.sync.dma_start(out=out_rows[:, PAIR * i : PAIR * (i + 1), :], in_=logits[:])
+        for s in range(PRODUCT_LAG, PAIRS + PRODUCT_LAG + 1):
+            step(s)
+            products(s - PRODUCT_LAG)
+            finish(s - PRODUCT_LAG - 1)

@@ -21,8 +21,9 @@ ROW_TILES = ROWS // P
 PAIR = 2
 PAIRS = ROW_TILES // PAIR
 EPS = 1e-8
-SCALAR_COLS = 640
-PRODUCT_LAG = 4
+QUANTISE_LAG = 4
+LAST_STAGE = QUANTISE_LAG + 2
+SCALAR_SQUARES = 3 * FREQS
 
 FLOPS = 2 * ROWS * P * (FEATURES + FREQS)
 
@@ -43,8 +44,9 @@ def tile_module2network_kernel(tc, K, reference_angles, probes, u_weights, k_bia
         k_pool = ctx.enter_context(tc.tile_pool(name="k_in", bufs=PAIRS))
         mx_pool = ctx.enter_context(tc.tile_pool(name="mx", bufs=PAIRS))
         work = ctx.enter_context(tc.tile_pool(name="work", bufs=3))
-        k_bank_pool = ctx.enter_context(tc.psum_pool(name="k_bank", bufs=2))
-        mag_bank_pool = ctx.enter_context(tc.psum_pool(name="mag_bank", bufs=4))
+        grouped_pool = ctx.enter_context(tc.tile_pool(name="grouped", bufs=QUANTISE_LAG + 2))
+        k_bank_pool = ctx.enter_context(tc.psum_pool(name="k_bank", bufs=4))
+        start_pool = ctx.enter_context(tc.psum_pool(name="start", bufs=2))
         acc_pool = ctx.enter_context(tc.psum_pool(name="acc", bufs=2))
         ctx.enter_context(tc.manual_schedule())
 
@@ -55,14 +57,14 @@ def tile_module2network_kernel(tc, K, reference_angles, probes, u_weights, k_bia
         )
         probes_sb = const.tile([P, FEATURES], BF16)
         nc.sync.dma_start(out=probes_sb[:], in_=probes)
+        u_sb = const.tile([P, FREQS], BF16)
+        nc.sync.dma_start(out=u_sb[:], in_=u_weights)
         k_rows = K.rearrange("(p j) k -> p j k", j=ROW_TILES)
         k_in = []
         for i in range(PAIRS):
             k_pair = k_pool.tile([P, PAIR, FEATURES], BF16, name="k_pair")
             k_in.append(k_pair)
         nc.sync.dma_start(out=k_in[0][:], in_=k_rows[:, 0:PAIR, :])
-        u_sb = const.tile([P, FREQS], BF16)
-        nc.sync.dma_start(out=u_sb[:], in_=u_weights)
         bias_rows = const.tile([P, P], BF16)
         nc.sync.dma_start(out=bias_rows[:], in_=k_bias.partition_broadcast(P))
         for i in range(1, PAIRS):
@@ -77,12 +79,12 @@ def tile_module2network_kernel(tc, K, reference_angles, probes, u_weights, k_bia
         eps_col = const.tile([P, 1], F32)
         nc.gpsimd.memset(eps_col[:], EPS)
 
-        k_squared = {}
         k_banks = {}
         k_grouped = {}
         k_codes = {}
         k_scales = {}
-        mag_banks = {}
+        k_squared = {}
+        mag_squared = {}
         mag_grouped = {}
         mag_codes = {}
         mag_scales = {}
@@ -92,22 +94,6 @@ def tile_module2network_kernel(tc, K, reference_angles, probes, u_weights, k_bia
 
         def exists(i):
             return 0 <= i < PAIRS
-
-        def squares(i):
-            if not exists(i):
-                return
-            k_squared[i] = work.tile([P, PAIR, FEATURES], F32, name="k_squared")
-            nc.scalar.activation(
-                out=k_squared[i][:, :, 0:SCALAR_COLS],
-                in_=k_in[i][:, :, 0:SCALAR_COLS],
-                func=ACT.Square,
-            )
-            nc.gpsimd.tensor_tensor(
-                out=k_squared[i][:, :, SCALAR_COLS:FEATURES],
-                in0=k_in[i][:, :, SCALAR_COLS:FEATURES],
-                in1=k_in[i][:, :, SCALAR_COLS:FEATURES],
-                op=ALU.mult,
-            )
 
         def turn_k(i):
             if not exists(i):
@@ -123,13 +109,24 @@ def tile_module2network_kernel(tc, K, reference_angles, probes, u_weights, k_bia
         def copy_k(i):
             if not exists(i):
                 return
-            k_grouped[i] = work.tile([P, PAIR, 2, P, PACK], BF16, align_bytes=64, name="k_grouped")
-            k_grouped_words = k_grouped[i][:].bitcast(F32)
-            for j in range(PAIR):
+            k_grouped[i] = grouped_pool.tile(
+                [P, PAIR, 2, P * PACK], BF16, align_bytes=64, name="k_grouped"
+            )
+            k_grouped_words = k_grouped[i][:].bitcast(F32).rearrange("p j g (n u) -> p j g n u", u=2)
+            for j in reversed(range(PAIR)):
                 nc.vector.tensor_copy(
                     out=k_grouped_words[:, j],
                     in_=k_banks[i][j][:].rearrange("p (g u) n -> p g n u", g=2),
                 )
+            k_squared[i] = work.tile([P, PAIR, 2, P * PACK], F32, name="k_squared")
+            nc.vector.tensor_tensor(
+                out=k_squared[i][:, PAIR - 1, 1, :].rearrange("p (n u e) -> p n u e", u=2, e=2),
+                in0=k_banks[i][PAIR - 1][:]
+                .bitcast(BF16)[:, 2:PACK, :]
+                .rearrange("p u (n e) -> p n u e", e=2),
+                in1=k_grouped[i][:, PAIR - 1, 1, :].rearrange("p (n u e) -> p n u e", u=2, e=2),
+                op=ALU.mult,
+            )
 
         def quantise_k(i):
             if not exists(i):
@@ -138,41 +135,38 @@ def tile_module2network_kernel(tc, K, reference_angles, probes, u_weights, k_bia
             k_scales[i] = mx_pool.tile([P, PAIR, 2, P], U8, align_bytes=64, name="k_scales")
             quantise(
                 nc,
-                k_grouped[i][:].rearrange("p j g n t -> p (j g n t)"),
+                k_grouped[i][:].rearrange("p j g w -> p (j g w)"),
                 k_codes[i][:].rearrange("p j g n -> p (j g n)"),
                 k_scales[i][:].rearrange("p j g n -> p (j g n)"),
             )
 
-        def turn_squares(i):
+        def squares(i):
             if not exists(i):
                 return
-            mag_banks[i] = []
-            for j in range(PAIR):
-                mag_bank = mag_bank_pool.tile([P, PACK, P], F32, tag="mag_bank", name="mag_bank")
-                for t in range(PACK):
-                    for g in range(2):
-                        first = FREQS * g + P * t
-                        nc.tensor.matmul(
-                            out=mag_bank[:, t, :],
-                            lhsT=k_squared[i][:, j, first : first + P],
-                            rhs=ident[:],
-                            is_transpose=True,
-                            start=(g == 0),
-                            stop=(g == 1),
-                        )
-                mag_banks[i].append(mag_bank)
+            nc.scalar.activation(
+                out=k_squared[i][:].rearrange("p j g w -> p (j g w)")[:, 0:SCALAR_SQUARES],
+                in_=k_grouped[i][:].rearrange("p j g w -> p (j g w)")[:, 0:SCALAR_SQUARES],
+                func=ACT.Square,
+            )
+
+        def sums(i):
+            if not exists(i):
+                return
+            mag_squared[i] = work.tile([P, PAIR, P * PACK], F32, name="mag_squared")
+            nc.gpsimd.tensor_tensor(
+                out=mag_squared[i][:],
+                in0=k_squared[i][:, :, 0, :],
+                in1=k_squared[i][:, :, 1, :],
+                op=ALU.add,
+            )
 
         def roots(i):
             if not exists(i):
                 return
-            mag_grouped[i] = work.tile([P, PAIR, P, PACK], BF16, align_bytes=64, name="mag_grouped")
-            for j in range(PAIR):
-                nc.scalar.activation(
-                    out=mag_grouped[i][:, j],
-                    in_=mag_banks[i][j][:].rearrange("p t n -> p n t"),
-                    func=ACT.Sqrt,
-                    bias=eps_col[:, 0:1],
-                )
+            mag_grouped[i] = work.tile([P, PAIR, P * PACK], BF16, align_bytes=64, name="mag_grouped")
+            nc.scalar.activation(
+                out=mag_grouped[i][:], in_=mag_squared[i][:], func=ACT.Sqrt, bias=eps_col[:, 0:1]
+            )
 
         def quantise_mag(i):
             if not exists(i):
@@ -181,7 +175,7 @@ def tile_module2network_kernel(tc, K, reference_angles, probes, u_weights, k_bia
             mag_scales[i] = mx_pool.tile([P, PAIR, P], U8, align_bytes=64, name="mag_scales")
             quantise(
                 nc,
-                mag_grouped[i][:].rearrange("p j n t -> p (j n t)"),
+                mag_grouped[i][:].rearrange("p j w -> p (j w)"),
                 mag_codes[i][:].rearrange("p j n -> p (j n)"),
                 mag_scales[i][:].rearrange("p j n -> p (j n)"),
             )
@@ -189,7 +183,7 @@ def tile_module2network_kernel(tc, K, reference_angles, probes, u_weights, k_bia
         def products(i):
             if not exists(i):
                 return
-            accs[i] = acc_pool.tile([P, PAIR, P], F32, tag="acc", name="acc")
+            accs[i] = acc_pool.tile([P, PAIR, P], F32, name="acc")
             for j in range(PAIR):
                 for g in range(2):
                     nc.tensor.matmul_mx(
@@ -219,14 +213,15 @@ def tile_module2network_kernel(tc, K, reference_angles, probes, u_weights, k_bia
             nc.sync.dma_start(out=out_rows[:, PAIR * i : PAIR * (i + 1), :], in_=logits[:])
 
         def step(s):
-            squares(s + 1)
-            turn_squares(s)
-            copy_k(s)
-            quantise_mag(s - 1)
             turn_k(s + 1)
-            quantise_k(s)
-            roots(s)
-
+            copy_k(s)
+            squares(s - 1)
+            sums(s - 2)
+            quantise_k(s - QUANTISE_LAG)
+            roots(s - 3)
+            quantise_mag(s - QUANTISE_LAG)
+            products(s - QUANTISE_LAG - 1)
+            finish(s - LAST_STAGE)
 
         angle = const.tile([P, 2 * PACK], F32)
         nc.vector.tensor_scalar(
@@ -282,21 +277,23 @@ def tile_module2network_kernel(tc, K, reference_angles, probes, u_weights, k_bia
         sin_b = sin_cos[:, 0:PACK].unsqueeze(2).to_broadcast([P, PACK, P])
         cos_b = sin_cos[:, PACK : 2 * PACK].unsqueeze(2).to_broadcast([P, PACK, P])
 
+        u_words = u_sb[:].bitcast(F32)
+        u_bank = start_pool.tile([P, PACK, P], F32, tag="start", name="u_bank")
+        for u in range(2):
+            nc.tensor.transpose(u_bank[:, u, :], u_words[:, P * u : P * (u + 1)], ident[:])
+        u_grouped = const.tile([P, P, PACK], BF16, align_bytes=64)
+        nc.vector.tensor_copy(
+            out=u_grouped[:].bitcast(F32), in_=u_bank[:, 0:2, :].rearrange("p u b -> p b u")
+        )
+        u_codes = const.tile([P, P], U32, align_bytes=64)
+        u_scales = const.tile([P, P], U8, align_bytes=64)
+        quantise(nc, u_grouped[:].rearrange("p b t -> p (b t)"), u_codes[:], u_scales[:])
+
         step(-1)
+        step(0)
 
         norm = const.tile([P, 1], F32)
         nc.scalar.activation(out=norm[:], in_=sum_squares[:], func=ACT.Sqrt)
-
-        step(0)
-
-        u_f32 = const.tile([P, FREQS], F32)
-        nc.gpsimd.tensor_scalar(
-            out=u_f32[:], in0=u_sb[:], scalar1=1.0, scalar2=0.0, op0=ALU.mult, op1=ALU.add
-        )
-        u_bank = mag_bank_pool.tile([P, PACK, P], F32, tag="mag_bank", name="u_bank")
-        for t in range(PACK):
-            nc.tensor.transpose(u_bank[:, t, :], u_f32[:, P * t : P * (t + 1)], ident[:])
-
         norm_eps = const.tile([P, 1], F32)
         nc.vector.tensor_scalar_add(out=norm_eps[:], in0=norm[:], scalar1=EPS)
         inv_norm = const.tile([P, 1], F32)
@@ -306,16 +303,11 @@ def tile_module2network_kernel(tc, K, reference_angles, probes, u_weights, k_bia
         p_cols = p_unit[:].rearrange("b (g u q e) -> b g u q e", g=2, u=2, e=2)
         p_turned = []
         for g in range(2):
-            p_bank = acc_pool.tile([P, PACK, P], F32, tag="acc", name="p_bank")
+            p_bank = start_pool.tile([P, PACK, P], F32, tag="start", name="p_bank")
             for u in range(2):
                 for e in range(2):
                     nc.tensor.transpose(p_bank[:, 2 * u + e, :], p_cols[:, g, u, :, e], ident[:])
             p_turned.append(p_bank)
-        u_grouped = const.tile([P, P, PACK], BF16, align_bytes=64)
-        nc.vector.tensor_copy(out=u_grouped[:], in_=u_bank[:].rearrange("p t b -> p b t"))
-        u_codes = const.tile([P, P], U32, align_bytes=64)
-        u_scales = const.tile([P, P], U8, align_bytes=64)
-        quantise(nc, u_grouped[:].rearrange("p b t -> p (b t)"), u_codes[:], u_scales[:])
 
         step(1)
 
@@ -323,28 +315,31 @@ def tile_module2network_kernel(tc, K, reference_angles, probes, u_weights, k_bia
         nc.vector.tensor_tensor(out=re_cos[:], in0=p_turned[0][:], in1=cos_b, op=ALU.mult)
         im_sin = const.tile([P, PACK, P], F32)
         nc.vector.tensor_tensor(out=im_sin[:], in0=p_turned[1][:], in1=sin_b, op=ALU.mult)
+
+        step(2)
+
         im_cos = const.tile([P, PACK, P], F32)
         nc.vector.tensor_tensor(out=im_cos[:], in0=p_turned[1][:], in1=cos_b, op=ALU.mult)
         re_sin = const.tile([P, PACK, P], F32)
         nc.vector.tensor_tensor(out=re_sin[:], in0=p_turned[0][:], in1=sin_b, op=ALU.mult)
 
-        step(2)
+        step(3)
 
         rot_grouped = const.tile([P, 2, P, PACK], BF16, align_bytes=64)
-        nc.gpsimd.tensor_tensor(
+        nc.vector.tensor_tensor(
             out=rot_grouped[:, 0],
             in0=re_cos[:].rearrange("p t b -> p b t"),
             in1=im_sin[:].rearrange("p t b -> p b t"),
             op=ALU.subtract,
         )
-        nc.gpsimd.tensor_tensor(
+        nc.vector.tensor_tensor(
             out=rot_grouped[:, 1],
             in0=im_cos[:].rearrange("p t b -> p b t"),
             in1=re_sin[:].rearrange("p t b -> p b t"),
             op=ALU.add,
         )
 
-        step(3)
+        step(4)
 
         rot_codes = const.tile([P, 2, P], U32, align_bytes=64)
         rot_scales = const.tile([P, 2, P], U8, align_bytes=64)
@@ -355,7 +350,5 @@ def tile_module2network_kernel(tc, K, reference_angles, probes, u_weights, k_bia
             rot_scales[:].rearrange("p g b -> p (g b)"),
         )
 
-        for s in range(PRODUCT_LAG, PAIRS + PRODUCT_LAG + 1):
+        for s in range(QUANTISE_LAG + 1, PAIRS + LAST_STAGE):
             step(s)
-            products(s - PRODUCT_LAG)
-            finish(s - PRODUCT_LAG - 1)

@@ -64,11 +64,9 @@ def tile_module2network_kernel(tc, K, reference_angles, probes, u_weights, k_bia
         for i in range(PAIRS):
             k_pair = k_pool.tile([P, PAIR, FEATURES], BF16, name="k_pair")
             k_in.append(k_pair)
-        nc.sync.dma_start(out=k_in[0][:], in_=k_rows[:, 0:PAIR, :])
+            nc.sync.dma_start(out=k_pair[:], in_=k_rows[:, PAIR * i : PAIR * (i + 1), :])
         bias_rows = const.tile([P, P], BF16)
         nc.sync.dma_start(out=bias_rows[:], in_=k_bias.partition_broadcast(P))
-        for i in range(1, PAIRS):
-            nc.sync.dma_start(out=k_in[i][:], in_=k_rows[:, PAIR * i : PAIR * (i + 1), :])
 
         zero_col = const.tile([P, 1], F32)
         nc.gpsimd.memset(zero_col[:], 0.0)

@@ -151,12 +151,13 @@ def tile_module2network_kernel(tc, K, reference_angles, probes, u_weights, k_bia
             if not exists(i):
                 return
             mag_squared[i] = work.tile([P, PAIR, P * PACK], F32, name="mag_squared")
-            nc.gpsimd.tensor_tensor(
-                out=mag_squared[i][:],
-                in0=k_squared[i][:, :, 0, :],
-                in1=k_squared[i][:, :, 1, :],
-                op=ALU.add,
-            )
+            for j in range(PAIR):
+                nc.gpsimd.tensor_tensor(
+                    out=mag_squared[i][:, j, :],
+                    in0=k_squared[i][:, j, 0, :],
+                    in1=k_squared[i][:, j, 1, :],
+                    op=ALU.add,
+                )
 
         def roots(i):
             if not exists(i):

@@ -16,7 +16,8 @@ P = 128
 PACK = 4
 ROWS = 3072
 FREQS = 512
-FEATURES = 2 * FREQS
+PARTS = 2
+FEATURES = PARTS * FREQS
 ROW_TILES = ROWS // P
 PAIR = 2
 PAIRS = ROW_TILES // PAIR
@@ -52,8 +53,8 @@ def tile_module2network_kernel(tc, K, reference_angles, probes, u_weights, k_bia
 
         theta = const.tile([P, PACK], BF16)
         nc.sync.dma_start(
-            out=theta[:].rearrange("p (u e) -> p u e", u=2),
-            in_=reference_angles.rearrange("(u p e) -> p u e", u=2, e=2),
+            out=theta[:].rearrange("p (h e) -> p h e", h=2),
+            in_=reference_angles.rearrange("(h p e) -> p h e", h=2, e=2),
         )
         probes_sb = const.tile([P, FEATURES], BF16)
         nc.sync.dma_start(out=probes_sb[:], in_=probes)
@@ -93,44 +94,44 @@ def tile_module2network_kernel(tc, K, reference_angles, probes, u_weights, k_bia
         def exists(i):
             return 0 <= i < PAIRS
 
-        def turn_k(i):
+        def transpose_k(i):
             if not exists(i):
                 return
             k_words = k_in[i][:].bitcast(F32)
-            k_banks[i] = []
-            for j in range(PAIR):
+            k_banks[i] = {}
+            for j in reversed(range(PAIR)):
                 k_bank = k_bank_pool.tile([P, PACK, P], F32, name="k_bank")
                 for c in range(PACK):
                     nc.tensor.transpose(k_bank[:, c, :], k_words[:, j, P * c : P * (c + 1)], ident[:])
-                k_banks[i].append(k_bank)
+                k_banks[i][j] = k_bank
 
         def copy_k(i):
             if not exists(i):
                 return
             k_grouped[i] = grouped_pool.tile(
-                [P, PAIR, 2, P * PACK], BF16, align_bytes=64, name="k_grouped"
+                [P, PAIR, PARTS, P * PACK], BF16, align_bytes=64, name="k_grouped"
             )
-            k_grouped_words = k_grouped[i][:].bitcast(F32).rearrange("p j g (n u) -> p j g n u", u=2)
+            k_grouped_words = k_grouped[i][:].bitcast(F32).rearrange("p j g (n h) -> p j g n h", h=2)
             for j in reversed(range(PAIR)):
                 nc.vector.tensor_copy(
                     out=k_grouped_words[:, j],
-                    in_=k_banks[i][j][:].rearrange("p (g u) n -> p g n u", g=2),
+                    in_=k_banks[i][j][:].rearrange("p (g h) n -> p g n h", g=PARTS),
                 )
-            k_squared[i] = work.tile([P, PAIR, 2, P * PACK], F32, name="k_squared")
+            k_squared[i] = work.tile([P, PAIR, PARTS, P * PACK], F32, name="k_squared")
             nc.vector.tensor_tensor(
-                out=k_squared[i][:, PAIR - 1, 1, :].rearrange("p (n u e) -> p n u e", u=2, e=2),
+                out=k_squared[i][:, PAIR - 1, 1, :].rearrange("p (n h e) -> p n h e", h=2, e=2),
                 in0=k_banks[i][PAIR - 1][:]
                 .bitcast(BF16)[:, 2:PACK, :]
-                .rearrange("p u (n e) -> p n u e", e=2),
-                in1=k_grouped[i][:, PAIR - 1, 1, :].rearrange("p (n u e) -> p n u e", u=2, e=2),
+                .rearrange("p h (n e) -> p n h e", e=2),
+                in1=k_grouped[i][:, PAIR - 1, 1, :].rearrange("p (n h e) -> p n h e", h=2, e=2),
                 op=ALU.mult,
             )
 
         def quantise_k(i):
             if not exists(i):
                 return
-            k_codes[i] = mx_pool.tile([P, PAIR, 2, P], U32, align_bytes=64, name="k_codes")
-            k_scales[i] = mx_pool.tile([P, PAIR, 2, P], U8, align_bytes=64, name="k_scales")
+            k_codes[i] = mx_pool.tile([P, PAIR, PARTS, P], U32, align_bytes=64, name="k_codes")
+            k_scales[i] = mx_pool.tile([P, PAIR, PARTS, P], U8, align_bytes=64, name="k_scales")
             quantise(
                 nc,
                 k_grouped[i][:].rearrange("p j g w -> p (j g w)"),
@@ -151,13 +152,12 @@ def tile_module2network_kernel(tc, K, reference_angles, probes, u_weights, k_bia
             if not exists(i):
                 return
             mag_squared[i] = work.tile([P, PAIR, P * PACK], F32, name="mag_squared")
-            for j in range(PAIR):
-                nc.gpsimd.tensor_tensor(
-                    out=mag_squared[i][:, j, :],
-                    in0=k_squared[i][:, j, 0, :],
-                    in1=k_squared[i][:, j, 1, :],
-                    op=ALU.add,
-                )
+            nc.gpsimd.tensor_tensor(
+                out=mag_squared[i][:],
+                in0=k_squared[i][:, :, 0, :],
+                in1=k_squared[i][:, :, 1, :],
+                op=ALU.add,
+            )
 
         def roots(i):
             if not exists(i):
@@ -184,7 +184,7 @@ def tile_module2network_kernel(tc, K, reference_angles, probes, u_weights, k_bia
                 return
             accs[i] = acc_pool.tile([P, PAIR, P], F32, name="acc")
             for j in range(PAIR):
-                for g in range(2):
+                for g in range(PARTS):
                     nc.tensor.matmul_mx(
                         out=accs[i][:, j, :],
                         lhsT=k_codes[i][:, j, g, :].bitcast(FP8X4),
@@ -212,7 +212,7 @@ def tile_module2network_kernel(tc, K, reference_angles, probes, u_weights, k_bia
             nc.sync.dma_start(out=out_rows[:, PAIR * i : PAIR * (i + 1), :], in_=logits[:])
 
         def step(s):
-            turn_k(s + 1)
+            transpose_k(s + 1)
             copy_k(s)
             squares(s - 1)
             sums(s - 2)
@@ -278,11 +278,11 @@ def tile_module2network_kernel(tc, K, reference_angles, probes, u_weights, k_bia
 
         u_words = u_sb[:].bitcast(F32)
         u_bank = start_pool.tile([P, PACK, P], F32, tag="start", name="u_bank")
-        for u in range(2):
-            nc.tensor.transpose(u_bank[:, u, :], u_words[:, P * u : P * (u + 1)], ident[:])
+        for h in range(2):
+            nc.tensor.transpose(u_bank[:, h, :], u_words[:, P * h : P * (h + 1)], ident[:])
         u_grouped = const.tile([P, P, PACK], BF16, align_bytes=64)
         nc.vector.tensor_copy(
-            out=u_grouped[:].bitcast(F32), in_=u_bank[:, 0:2, :].rearrange("p u b -> p b u")
+            out=u_grouped[:].bitcast(F32), in_=u_bank[:, 0:2, :].rearrange("p h b -> p b h")
         )
         u_codes = const.tile([P, P], U32, align_bytes=64)
         u_scales = const.tile([P, P], U8, align_bytes=64)
@@ -299,32 +299,32 @@ def tile_module2network_kernel(tc, K, reference_angles, probes, u_weights, k_bia
         nc.vector.reciprocal(out=inv_norm[:], in_=norm_eps[:])
         p_unit = const.tile([P, FEATURES], F32)
         nc.vector.tensor_scalar_mul(out=p_unit[:], in0=probes_sb[:], scalar1=inv_norm[:, 0:1])
-        p_cols = p_unit[:].rearrange("b (g u q e) -> b g u q e", g=2, u=2, e=2)
-        p_turned = []
-        for g in range(2):
+        p_cols = p_unit[:].rearrange("b (g h q e) -> b g h q e", g=PARTS, h=2, e=2)
+        p_banks = []
+        for g in range(PARTS):
             p_bank = start_pool.tile([P, PACK, P], F32, tag="start", name="p_bank")
-            for u in range(2):
+            for h in range(2):
                 for e in range(2):
-                    nc.tensor.transpose(p_bank[:, 2 * u + e, :], p_cols[:, g, u, :, e], ident[:])
-            p_turned.append(p_bank)
+                    nc.tensor.transpose(p_bank[:, 2 * h + e, :], p_cols[:, g, h, :, e], ident[:])
+            p_banks.append(p_bank)
 
         step(1)
 
         re_cos = const.tile([P, PACK, P], F32)
-        nc.vector.tensor_tensor(out=re_cos[:], in0=p_turned[0][:], in1=cos_b, op=ALU.mult)
+        nc.vector.tensor_tensor(out=re_cos[:], in0=p_banks[0][:], in1=cos_b, op=ALU.mult)
         im_sin = const.tile([P, PACK, P], F32)
-        nc.vector.tensor_tensor(out=im_sin[:], in0=p_turned[1][:], in1=sin_b, op=ALU.mult)
+        nc.vector.tensor_tensor(out=im_sin[:], in0=p_banks[1][:], in1=sin_b, op=ALU.mult)
 
         step(2)
 
         im_cos = const.tile([P, PACK, P], F32)
-        nc.vector.tensor_tensor(out=im_cos[:], in0=p_turned[1][:], in1=cos_b, op=ALU.mult)
+        nc.vector.tensor_tensor(out=im_cos[:], in0=p_banks[1][:], in1=cos_b, op=ALU.mult)
         re_sin = const.tile([P, PACK, P], F32)
-        nc.vector.tensor_tensor(out=re_sin[:], in0=p_turned[0][:], in1=sin_b, op=ALU.mult)
+        nc.vector.tensor_tensor(out=re_sin[:], in0=p_banks[0][:], in1=sin_b, op=ALU.mult)
 
         step(3)
 
-        rot_grouped = const.tile([P, 2, P, PACK], BF16, align_bytes=64)
+        rot_grouped = const.tile([P, PARTS, P, PACK], BF16, align_bytes=64)
         nc.vector.tensor_tensor(
             out=rot_grouped[:, 0],
             in0=re_cos[:].rearrange("p t b -> p b t"),
@@ -340,8 +340,8 @@ def tile_module2network_kernel(tc, K, reference_angles, probes, u_weights, k_bia
 
         step(4)
 
-        rot_codes = const.tile([P, 2, P], U32, align_bytes=64)
-        rot_scales = const.tile([P, 2, P], U8, align_bytes=64)
+        rot_codes = const.tile([P, PARTS, P], U32, align_bytes=64)
+        rot_scales = const.tile([P, PARTS, P], U8, align_bytes=64)
         quantise(
             nc,
             rot_grouped[:].rearrange("p g b t -> p (g b t)"),

import math
from contextlib import ExitStack

import concourse.mybir as mybir
from concourse.masks import make_identity

F32 = mybir.dt.float32
BF16 = mybir.dt.bfloat16
U32 = mybir.dt.uint32
U8 = mybir.dt.uint8
FP8X4 = mybir.dt.float8_e4m3fn_x4
ACT = mybir.ActivationFunctionType
ALU = mybir.AluOpType

P = 128
PACK = 4
ROWS = 3072
FREQS = 512
PARTS = 2
FEATURES = PARTS * FREQS
ROW_TILES = ROWS // P
PAIR = 2
PAIRS = ROW_TILES // PAIR
EPS = 1e-8
QUANTISE_LAG = 4
LAST_STAGE = QUANTISE_LAG + 2
SCALAR_SQUARES = 3 * FREQS

FLOPS = 2 * ROWS * P * (FEATURES + FREQS)

TWO_PI = 2.0 * math.pi
TWO_PI_HIGH = 6.28125
TWO_PI_LOW = TWO_PI - TWO_PI_HIGH
ROUND_MAGIC = 1.5 * 2.0**23


def quantise(nc, values, codes, scales):
    nc.vector.quantize_mx(out=codes.bitcast(FP8X4), scales=scales, in_=values)


def tile_module2network_kernel(tc, K, reference_angles, probes, u_weights, k_bias, out):
    nc = tc.nc
    with ExitStack() as ctx:
        const = ctx.enter_context(tc.tile_pool(name="const", bufs=1))
        k_pool = ctx.enter_context(tc.tile_pool(name="k_in", bufs=PAIRS))
        mx_pool = ctx.enter_context(tc.tile_pool(name="mx", bufs=PAIRS))
        work = ctx.enter_context(tc.tile_pool(name="work", bufs=3))
        grouped_pool = ctx.enter_context(tc.tile_pool(name="grouped", bufs=QUANTISE_LAG + 2))
        k_bank_pool = ctx.enter_context(tc.psum_pool(name="k_bank", bufs=4))
        start_pool = ctx.enter_context(tc.psum_pool(name="start", bufs=2))
        acc_pool = ctx.enter_context(tc.psum_pool(name="acc", bufs=2))
        ctx.enter_context(tc.manual_schedule())

        theta = const.tile([P, PACK], BF16)
        nc.sync.dma_start(
            out=theta[:].rearrange("p (h e) -> p h e", h=2),
            in_=reference_angles.rearrange("(h p e) -> p h e", h=2, e=2),
        )
        probes_sb = const.tile([P, FEATURES], BF16)
        nc.sync.dma_start(out=probes_sb[:], in_=probes)
        u_sb = const.tile([P, FREQS], BF16)
        nc.sync.dma_start(out=u_sb[:], in_=u_weights)
        k_rows = K.rearrange("(p j) k -> p j k", j=ROW_TILES)
        k_in = []
        for i in range(PAIRS):
            k_pair = k_pool.tile([P, PAIR, FEATURES], BF16, name="k_pair")
            k_in.append(k_pair)
            nc.sync.dma_start(out=k_pair[:], in_=k_rows[:, PAIR * i : PAIR * (i + 1), :])
        bias_rows = const.tile([P, P], BF16)
        nc.sync.dma_start(out=bias_rows[:], in_=k_bias.partition_broadcast(P))

        zero_col = const.tile([P, 1], F32)
        nc.gpsimd.memset(zero_col[:], 0.0)
        warm_col = const.tile([P, 1], F32)
        nc.scalar.activation(out=warm_col[:], in_=zero_col[:], func=ACT.Sin)
        ident = const.tile([P, P], F32)
        make_identity(nc, ident[:])
        eps_col = const.tile([P, 1], F32)
        nc.gpsimd.memset(eps_col[:], EPS)

        k_banks = {}
        k_grouped = {}
        k_codes = {}
        k_scales = {}
        k_squared = {}
        mag_squared = {}
        mag_grouped = {}
        mag_codes = {}
        mag_scales = {}
        accs = {}
        out_rows = out.rearrange("(p j) b -> p j b", j=ROW_TILES)
        bias_b = bias_rows[:].unsqueeze(1).to_broadcast([P, PAIR, P])

        def exists(i):
            return 0 <= i < PAIRS

        def transpose_k(i):
            if not exists(i):
                return
            k_words = k_in[i][:].bitcast(F32)
            k_banks[i] = {}
            for j in reversed(range(PAIR)):
                k_bank = k_bank_pool.tile([P, PACK, P], F32, name="k_bank")
                for c in range(PACK):
                    nc.tensor.transpose(k_bank[:, c, :], k_words[:, j, P * c : P * (c + 1)], ident[:])
                k_banks[i][j] = k_bank

        def copy_k(i):
            if not exists(i):
                return
            k_grouped[i] = grouped_pool.tile(
                [P, PAIR, PARTS, P * PACK], BF16, align_bytes=64, name="k_grouped"
            )
            k_grouped_words = k_grouped[i][:].bitcast(F32).rearrange("p j g (n h) -> p j g n h", h=2)
            for j in reversed(range(PAIR)):
                nc.vector.tensor_copy(
                    out=k_grouped_words[:, j],
                    in_=k_banks[i][j][:].rearrange("p (g h) n -> p g n h", g=PARTS),
                )
            k_squared[i] = work.tile([P, PAIR, PARTS, P * PACK], F32, name="k_squared")
            nc.vector.tensor_tensor(
                out=k_squared[i][:, PAIR - 1, 1, :].rearrange("p (n h e) -> p n h e", h=2, e=2),
                in0=k_banks[i][PAIR - 1][:]
                .bitcast(BF16)[:, 2:PACK, :]
                .rearrange("p h (n e) -> p n h e", e=2),
                in1=k_grouped[i][:, PAIR - 1, 1, :].rearrange("p (n h e) -> p n h e", h=2, e=2),
                op=ALU.mult,
            )

        def quantise_k(i):
            if not exists(i):
                return
            k_codes[i] = mx_pool.tile([P, PAIR, PARTS, P], U32, align_bytes=64, name="k_codes")
            k_scales[i] = mx_pool.tile([P, PAIR, PARTS, P], U8, align_bytes=64, name="k_scales")
            quantise(
                nc,
                k_grouped[i][:].rearrange("p j g w -> p (j g w)"),
                k_codes[i][:].rearrange("p j g n -> p (j g n)"),
                k_scales[i][:].rearrange("p j g n -> p (j g n)"),
            )

        def squares(i):
            if not exists(i):
                return
            nc.scalar.activation(
                out=k_squared[i][:].rearrange("p j g w -> p (j g w)")[:, 0:SCALAR_SQUARES],
                in_=k_grouped[i][:].rearrange("p j g w -> p (j g w)")[:, 0:SCALAR_SQUARES],
                func=ACT.Square,
            )

        def sums(i):
            if not exists(i):
                return
            mag_squared[i] = work.tile([P, PAIR, P * PACK], F32, name="mag_squared")
            nc.gpsimd.tensor_tensor(
                out=mag_squared[i][:],
                in0=k_squared[i][:, :, 0, :],
                in1=k_squared[i][:, :, 1, :],
                op=ALU.add,
            )

        def roots(i):
            if not exists(i):
                return
            mag_grouped[i] = work.tile([P, PAIR, P * PACK], BF16, align_bytes=64, name="mag_grouped")
            nc.scalar.activation(
                out=mag_grouped[i][:], in_=mag_squared[i][:], func=ACT.Sqrt, bias=eps_col[:, 0:1]
            )

        def quantise_mag(i):
            if not exists(i):
                return
            mag_codes[i] = mx_pool.tile([P, PAIR, P], U32, align_bytes=64, name="mag_codes")
            mag_scales[i] = mx_pool.tile([P, PAIR, P], U8, align_bytes=64, name="mag_scales")
            quantise(
                nc,
                mag_grouped[i][:].rearrange("p j w -> p (j w)"),
                mag_codes[i][:].rearrange("p j n -> p (j n)"),
                mag_scales[i][:].rearrange("p j n -> p (j n)"),
            )

        def products(i):
            if not exists(i):
                return
            accs[i] = acc_pool.tile([P, PAIR, P], F32, name="acc")
            for j in range(PAIR):
                for g in range(PARTS):
                    nc.tensor.matmul_mx(
                        out=accs[i][:, j, :],
                        lhsT=k_codes[i][:, j, g, :].bitcast(FP8X4),
                        lhsT_scale=k_scales[i][:, j, g, :],
                        rhs=rot_codes[:, g, :].bitcast(FP8X4),
                        rhs_scale=rot_scales[:, g, :],
                        start=(g == 0),
                        stop=False,
                    )
                nc.tensor.matmul_mx(
                    out=accs[i][:, j, :],
                    lhsT=mag_codes[i][:, j, :].bitcast(FP8X4),
                    lhsT_scale=mag_scales[i][:, j, :],
                    rhs=u_codes[:].bitcast(FP8X4),
                    rhs_scale=u_scales[:],
                    start=False,
                    stop=True,
                )

        def finish(i):
            if not exists(i):
                return
            logits = work.tile([P, PAIR, P], F32, name="logits")
            nc.vector.tensor_tensor(out=logits[:], in0=accs[i][:], in1=bias_b, op=ALU.add)
            nc.sync.dma_start(out=out_rows[:, PAIR * i : PAIR * (i + 1), :], in_=logits[:])

        def step(s):
            transpose_k(s + 1)
            copy_k(s)
            squares(s - 1)
            sums(s - 2)
            quantise_k(s - QUANTISE_LAG)
            roots(s - 3)
            quantise_mag(s - QUANTISE_LAG)
            products(s - QUANTISE_LAG - 1)
            finish(s - LAST_STAGE)

        angle = const.tile([P, 2 * PACK], F32)
        nc.vector.tensor_scalar(
            out=angle[:, 0:PACK], in0=theta[:], scalar1=1.0, scalar2=0.0, op0=ALU.mult, op1=ALU.add
        )
        nc.vector.tensor_scalar(
            out=angle[:, PACK : 2 * PACK],
            in0=theta[:],
            scalar1=1.0,
            scalar2=0.5 * math.pi,
            op0=ALU.mult,
            op1=ALU.add,
        )
        turns = const.tile([P, 2 * PACK], F32)
        nc.vector.tensor_scalar(
            out=turns[:],
            in0=angle[:],
            scalar1=1.0 / TWO_PI,
            scalar2=ROUND_MAGIC,
            op0=ALU.mult,
            op1=ALU.add,
        )
        off_high = const.tile([P, 2 * PACK], F32)
        nc.vector.tensor_scalar(
            out=off_high[:],
            in0=turns[:],
            scalar1=-ROUND_MAGIC,
            scalar2=-TWO_PI_HIGH,
            op0=ALU.add,
            op1=ALU.mult,
        )
        off_low = const.tile([P, 2 * PACK], F32)
        nc.vector.tensor_scalar(
            out=off_low[:],
            in0=turns[:],
            scalar1=-ROUND_MAGIC,
            scalar2=-TWO_PI_LOW,
            op0=ALU.add,
            op1=ALU.mult,
        )
        reduced_high = const.tile([P, 2 * PACK], F32)
        nc.vector.tensor_tensor(out=reduced_high[:], in0=angle[:], in1=off_high[:], op=ALU.add)
        reduced = const.tile([P, 2 * PACK], F32)
        nc.vector.tensor_tensor(out=reduced[:], in0=reduced_high[:], in1=off_low[:], op=ALU.add)

        probes_squared = const.tile([P, FEATURES], BF16)
        sum_squares = const.tile([P, 1], F32)
        nc.scalar.activation(
            out=probes_squared[:], in_=probes_sb[:], func=ACT.Square, accum_out=sum_squares[:]
        )
        sin_cos = const.tile([P, 2 * PACK], F32)
        nc.scalar.activation(out=sin_cos[:], in_=reduced[:], func=ACT.Sin)
        sin_b = sin_cos[:, 0:PACK].unsqueeze(2).to_broadcast([P, PACK, P])
        cos_b = sin_cos[:, PACK : 2 * PACK].unsqueeze(2).to_broadcast([P, PACK, P])

        u_words = u_sb[:].bitcast(F32)
        u_bank = start_pool.tile([P, PACK, P], F32, tag="start", name="u_bank")
        for h in range(2):
            nc.tensor.transpose(u_bank[:, h, :], u_words[:, P * h : P * (h + 1)], ident[:])
        u_grouped = const.tile([P, P, PACK], BF16, align_bytes=64)
        nc.vector.tensor_copy(
            out=u_grouped[:].bitcast(F32), in_=u_bank[:, 0:2, :].rearrange("p h b -> p b h")
        )
        u_codes = const.tile([P, P], U32, align_bytes=64)
        u_scales = const.tile([P, P], U8, align_bytes=64)
        quantise(nc, u_grouped[:].rearrange("p b t -> p (b t)"), u_codes[:], u_scales[:])

        step(-1)
        step(0)

        norm = const.tile([P, 1], F32)
        nc.scalar.activation(out=norm[:], in_=sum_squares[:], func=ACT.Sqrt)
        norm_eps = const.tile([P, 1], F32)
        nc.vector.tensor_scalar_add(out=norm_eps[:], in0=norm[:], scalar1=EPS)
        inv_norm = const.tile([P, 1], F32)
        nc.vector.reciprocal(out=inv_norm[:], in_=norm_eps[:])
        p_unit = const.tile([P, FEATURES], F32)
        nc.vector.tensor_scalar_mul(out=p_unit[:], in0=probes_sb[:], scalar1=inv_norm[:, 0:1])
        p_cols = p_unit[:].rearrange("b (g h q e) -> b g h q e", g=PARTS, h=2, e=2)
        p_banks = []
        for g in range(PARTS):
            p_bank = start_pool.tile([P, PACK, P], F32, tag="start", name="p_bank")
            for h in range(2):
                for e in range(2):
                    nc.tensor.transpose(p_bank[:, 2 * h + e, :], p_cols[:, g, h, :, e], ident[:])
            p_banks.append(p_bank)

        step(1)

        re_cos = const.tile([P, PACK, P], F32)
        nc.vector.tensor_tensor(out=re_cos[:], in0=p_banks[0][:], in1=cos_b, op=ALU.mult)
        im_sin = const.tile([P, PACK, P], F32)
        nc.vector.tensor_tensor(out=im_sin[:], in0=p_banks[1][:], in1=sin_b, op=ALU.mult)

        step(2)

        im_cos = const.tile([P, PACK, P], F32)
        nc.vector.tensor_tensor(out=im_cos[:], in0=p_banks[1][:], in1=cos_b, op=ALU.mult)
        re_sin = const.tile([P, PACK, P], F32)
        nc.vector.tensor_tensor(out=re_sin[:], in0=p_banks[0][:], in1=sin_b, op=ALU.mult)

        step(3)

        rot_grouped = const.tile([P, PARTS, P, PACK], BF16, align_bytes=64)
        nc.vector.tensor_tensor(
            out=rot_grouped[:, 0],
            in0=re_cos[:].rearrange("p t b -> p b t"),
            in1=im_sin[:].rearrange("p t b -> p b t"),
            op=ALU.subtract,
        )
        nc.vector.tensor_tensor(
            out=rot_grouped[:, 1],
            in0=im_cos[:].rearrange("p t b -> p b t"),
            in1=re_sin[:].rearrange("p t b -> p b t"),
            op=ALU.add,
        )

        step(4)

        rot_codes = const.tile([P, PARTS, P], U32, align_bytes=64)
        rot_scales = const.tile([P, PARTS, P], U8, align_bytes=64)
        quantise(
            nc,
            rot_grouped[:].rearrange("p g b t -> p (g b t)"),
            rot_codes[:].rearrange("p g b -> p (g b)"),
            rot_scales[:].rearrange("p g b -> p (g b)"),
        )

        for s in range(QUANTISE_LAG + 1, PAIRS + LAST_STAGE):
            step(s)
